import numpy as np
import ml_dtypes


def mxq(x, axis, fmt="e4m3"):
    dtype, down = {"e4m3": (ml_dtypes.float8_e4m3fn, 7), "e5m2": (ml_dtypes.float8_e5m2, 14)}[fmt]
    v = np.moveaxis(np.asarray(x, np.float32).astype(ml_dtypes.bfloat16).astype(np.float64), axis, -1)
    blocks = v.reshape(v.shape[:-1] + (-1, 32))
    amax = np.abs(blocks).max(-1, keepdims=True)
    byte = np.maximum(np.where(amax > 0, np.frexp(amax)[1] - 1 + 127, 0) - down, 1)
    scale = np.exp2(byte - 127.0)
    codes = (blocks / scale).astype(np.float32).astype(dtype).astype(np.float64)
    return np.moveaxis((codes * scale).reshape(v.shape), -1, axis)


WIDE = False


def mx_kscale(k):
    if not WIDE:
        return np.ones(k)
    levels = np.array([10, -10, 5, -5, 0])
    a = np.random.permutation(np.resize(levels, k // 512 * 4)).reshape(k // 512, 4)
    idx = np.arange(k)
    return np.exp2(a[idx // 512, idx % 128 // 32])


BF16 = ml_dtypes.bfloat16


def bf(x):
    return np.asarray(x, np.float32).astype(BF16)


def f64(x):
    return np.asarray(x).astype(np.float64)


B, N, F, G, K = 64, 128, 512, 512, 2048
EPS = 1e-8


def setup_inputs():
    s = mx_kscale(F)
    a = np.random.standard_normal((B, N, 1))
    g = np.random.standard_normal((B, 1, F))
    h = 2.0 * (np.random.standard_normal((B, N, F)) + a * g)
    w = (np.random.standard_normal((F, G)) + 0.5 * np.random.standard_normal((F, 1))) / np.sqrt(F)
    return {"h": bf(h * s), "W_h": bf(w / s[:, None]), "beta": bf(2.0 + np.random.uniform(size=1))}


def reference(h, W_h, beta):
    Wh = mxq(f64(h), 2, "e4m3") @ mxq(f64(W_h), 0, "e4m3")
    xm = Wh - Wh.mean(-1, keepdims=True)
    xq = mxq(xm, 2, "e4m3")
    cov = xq @ xq.transpose(0, 2, 1)
    norm = np.sqrt((xm * xm).sum(-1))
    denom = norm[:, :, None] * norm[:, None, :] + EPS
    return f64(beta) * np.abs(cov / denom)

@@ -1,0 +1,247 @@
+from contextlib import ExitStack
+
+import concourse.mybir as mybir
+from concourse.masks import make_identity
+
+F32 = mybir.dt.float32
+BF16 = mybir.dt.bfloat16
+U32 = mybir.dt.uint32
+U8 = mybir.dt.uint8
+FP8X4 = mybir.dt.float8_e4m3fn_x4
+ACT = mybir.ActivationFunctionType
+ALU = mybir.AluOpType
+
+GRAPHS = 64
+P = 128
+F_IN = 512
+F_OUT = 512
+PACK = 4
+HALVES = 2
+PAIR = 2
+N_PAIRS = GRAPHS // PAIR
+LOAD_AHEAD = 4
+EPS = 1e-8
+TINY = 1e-30
+
+FLOPS = 2 * GRAPHS * P * F_IN * F_OUT + 2 * GRAPHS * P * P * F_OUT
+
+
+def tile_pearsonattention_pa_t_kernel(tc, h, W_h, beta, out):
+    nc = tc.nc
+    with ExitStack() as ctx:
+        keep = ctx.enter_context(tc.tile_pool(name="keep", bufs=1))
+        work = ctx.enter_context(tc.tile_pool(name="work", bufs=3))
+        small = ctx.enter_context(tc.tile_pool(name="small", bufs=8))
+        psum = ctx.enter_context(tc.psum_pool(name="psum", bufs=1))
+        ctx.enter_context(tc.manual_schedule())
+
+        h_all = keep.tile([P, GRAPHS, F_IN], BF16)
+        w_raw = keep.tile([P, PACK, F_OUT], BF16)
+        beta_bf = keep.tile([P, 1], BF16)
+
+        def load_pair(r):
+            graphs = slice(PAIR * r, PAIR * (r + 1))
+            nc.sync.dma_start(out=h_all[:, graphs, :], in_=h[graphs].rearrange("b n k -> n b k"))
+
+        load_pair(0)
+        for u in range(HALVES):
+            rows = W_h[256 * u : 256 * (u + 1), :]
+            nc.sync.dma_start(
+                out=w_raw[:, 2 * u : 2 * u + 2, :], in_=rows.rearrange("(p e) c -> p e c", e=2)
+            )
+        for r in range(1, LOAD_AHEAD):
+            load_pair(r)
+        nc.sync.dma_start(out=beta_bf[:], in_=beta.partition_broadcast(P))
+
+        ident = keep.tile([P, P], F32)
+        make_identity(nc, ident[:])
+
+        w_grouped = keep.tile([P, F_OUT, PACK], BF16, align_bytes=64)
+        w_codes = keep.tile([P, F_OUT], U32, align_bytes=64)
+        w_scales = keep.tile([P, F_OUT], U8, align_bytes=64)
+        nc.vector.tensor_copy(out=w_grouped[:], in_=w_raw[:].rearrange("p t c -> p c t"))
+        nc.vector.quantize_mx(
+            out=w_codes[:].bitcast(FP8X4),
+            scales=w_scales[:],
+            in_=w_grouped[:].rearrange("p c t -> p (c t)"),
+        )
+        beta_f = keep.tile([P, 1], F32)
+        nc.vector.tensor_copy(out=beta_f[:], in_=beta_bf[:])
+
+        hT, h_grouped, h_q = {}, {}, {}
+        x, moments, negmean, xm = {}, {}, {}, {}
+        rsqrt_sum, norm = {}, {}
+        xT, x_grouped, x_q = {}, {}, {}
+        spread_cov, scale_abs = {}, {}
+
+        def transpose_words(dst, src):
+            for j in range(PAIR):
+                words = src[:, j, :].bitcast(F32)
+                for u in range(HALVES):
+                    nc.tensor.transpose(dst[:, j, u, :], words[:, P * u : P * (u + 1)], ident[:])
+
+        def quantise(grouped, name):
+            codes = work.tile([P, PAIR, P], U32, name=name + "_codes", align_bytes=64)
+            scales = work.tile([P, PAIR, P], U8, name=name + "_scales", align_bytes=64)
+            nc.vector.quantize_mx(
+                out=codes[:].rearrange("p j n -> p (j n)").bitcast(FP8X4),
+                scales=scales[:].rearrange("p j n -> p (j n)"),
+                in_=grouped[:].rearrange("p j n t -> p (j n t)"),
+            )
+            return codes, scales
+
+        def transpose_h(r):
+            hT[r] = psum.tile([P, PAIR, HALVES, P], F32, name="hT")
+            transpose_words(hT[r], h_all[:, PAIR * r : PAIR * (r + 1), :])
+
+        def copy_hT(r):
+            h_grouped[r] = work.tile([P, PAIR, P, PACK], BF16, name="h_grouped", align_bytes=64)
+            nc.scalar.copy(
+                out=h_grouped[r][:].bitcast(F32), in_=hT[r][:].rearrange("p j u n -> p j n u")
+            )
+
+        def quantise_h(r):
+            h_q[r] = quantise(h_grouped[r], "h")
+
+        def project(r):
+            codes, scales = h_q[r]
+            x[r] = []
+            for j in range(PAIR):
+                x_j = psum.tile([P, F_OUT], F32, name="x", bufs=2 * PAIR)
+                nc.tensor.matmul_mx(
+                    out=x_j[:],
+                    lhsT=codes[:, j, :].bitcast(FP8X4),
+                    lhsT_scale=scales[:, j, :],
+                    rhs=w_codes[:].bitcast(FP8X4),
+                    rhs_scale=w_scales[:],
+                    start=True,
+                    stop=True,
+                )
+                x[r].append(x_j)
+
+        def statistics(r):
+            parts = small.tile([P, PAIR, 6], F32, name="parts")
+            moments[r] = small.tile([P, PAIR, 2], F32, name="moments")
+            negmean[r] = small.tile([P, PAIR], F32, name="negmean")
+            for j in range(PAIR):
+                nc.vector.bn_stats(out=parts[:, j, :], in_=x[r][j][:])
+            for j in range(PAIR):
+                nc.vector.bn_aggr(out=moments[r][:, j, :], in_=parts[:, j, :])
+            nc.vector.tensor_scalar(
+                out=negmean[r][:], in0=moments[r][:, :, 0], scalar1=-1.0, scalar2=None, op0=ALU.mult
+            )
+
+        def subtract_mean(r):
+            xm[r] = work.tile([P, PAIR, F_OUT], BF16, name="xm")
+            for j in range(PAIR):
+                nc.scalar.activation(
+                    out=xm[r][:, j, :],
+                    in_=x[r][j][:],
+                    func=ACT.Identity,
+                    bias=negmean[r][:, j : j + 1],
+                    scale=1.0,
+                )
+
+        def rsqrt_sums(r):
+            rsqrt_sum[r] = small.tile([P, PAIR], F32, name="rsqrt_sum")
+            nc.scalar.activation(
+                out=rsqrt_sum[r][:],
+                in_=moments[r][:, :, 1],
+                func=ACT.Abs_reciprocal_sqrt,
+                bias=TINY,
+                scale=float(F_OUT),
+            )
+
+        def norms(r):
+            norm[r] = small.tile([P, PAIR], F32, name="norm")
+            nc.vector.scalar_tensor_tensor(
+                out=norm[r][:],
+                in0=moments[r][:, :, 1],
+                scalar=float(F_OUT),
+                in1=rsqrt_sum[r][:],
+                op0=ALU.mult,
+                op1=ALU.mult,
+            )
+
+        def transpose_xm(r):
+            xT[r] = psum.tile([P, PAIR, HALVES, P], F32, name="xT")
+            transpose_words(xT[r], xm[r])
+
+        def copy_xT(r):
+            x_grouped[r] = work.tile([P, PAIR, P, PACK], BF16, name="x_grouped", align_bytes=64)
+            nc.vector.tensor_copy(
+                out=x_grouped[r][:].bitcast(F32), in_=xT[r][:].rearrange("p j u n -> p j n u")
+            )
+
+        def quantise_xm(r):
+            x_q[r] = quantise(x_grouped[r], "x")
+
+        def correlate(r):
+            codes, scales = x_q[r]
+            spread_cov[r] = psum.tile([P, 2, PAIR, P], F32, name="spread_cov", bufs=2)
+            for j in range(PAIR):
+                nc.tensor.matmul_mx(
+                    out=spread_cov[r][:, 1, j, :],
+                    lhsT=codes[:, j, :].bitcast(FP8X4),
+                    lhsT_scale=scales[:, j, :],
+                    rhs=codes[:, j, :].bitcast(FP8X4),
+                    rhs_scale=scales[:, j, :],
+                    start=True,
+                    stop=True,
+                )
+            for j in range(PAIR):
+                nc.tensor.transpose(
+                    spread_cov[r][:, 0, j, :], norm[r][:, j : j + 1].to_broadcast([P, P]), ident[:]
+                )
+
+        def denominators(r):
+            root = work.tile([P, PAIR, P], F32, name="root")
+            inverse = work.tile([P, PAIR, P], F32, name="inverse")
+            cov_abs = work.tile([P, PAIR, P], F32, name="cov_abs")
+            for j in range(PAIR):
+                nc.scalar.activation(
+                    out=root[:, j, :],
+                    in_=spread_cov[r][:, 0, j, :],
+                    func=ACT.Abs_reciprocal_sqrt,
+                    bias=EPS,
+                    scale=norm[r][:, j : j + 1],
+                )
+            nc.scalar.activation(out=cov_abs[:], in_=spread_cov[r][:, 1, :, :], func=ACT.Abs)
+            nc.scalar.activation(out=inverse[:], in_=root[:], func=ACT.Square)
+            scale_abs[r] = (inverse, cov_abs)
+
+        def scale_and_store(r):
+            inverse, cov_abs = scale_abs[r]
+            result = work.tile([P, PAIR, P], F32, name="result")
+            nc.vector.scalar_tensor_tensor(
+                out=result[:].rearrange("p j m -> p (j m)"),
+                in0=cov_abs[:].rearrange("p j m -> p (j m)"),
+                scalar=beta_f[:, 0:1],
+                in1=inverse[:].rearrange("p j m -> p (j m)"),
+                op0=ALU.mult,
+                op1=ALU.mult,
+            )
+            graphs = slice(PAIR * r, PAIR * (r + 1))
+            nc.sync.dma_start(out=out[graphs].rearrange("b n m -> n b m"), in_=result[:])
+
+        def run(stage, r):
+            if 0 <= r < N_PAIRS:
+                stage(r)
+
+        LAST_LAG = 4
+        for step in range(N_PAIRS + LAST_LAG):
+            run(load_pair, step + LOAD_AHEAD)
+            run(correlate, step - 4)
+            run(transpose_xm, step - 3)
+            run(copy_hT, step - 1)
+            run(transpose_h, step)
+            run(statistics, step - 2)
+            run(quantise_h, step - 1)
+            run(project, step - 1)
+            run(rsqrt_sums, step - 3)
+            run(denominators, step - 4)
+            run(subtract_mean, step - 2)
+            run(copy_xT, step - 3)
+            run(norms, step - 3)
+            run(scale_and_store, step - LAST_LAG)
+            run(quantise_xm, step - 3)

@@ -190,8 +190,12 @@ def tile_pearsonattention_pa_t_kernel(tc, h, W_h, beta, out):
                     stop=True,
                 )
             for j in range(PAIR):
-                nc.tensor.transpose(
-                    spread_cov[r][:, 0, j, :], norm[r][:, j : j + 1].to_broadcast([P, P]), ident[:]
+                nc.tensor.matmul(
+                    out=spread_cov[r][:, 0, j, :],
+                    lhsT=norm[r][:, j : j + 1].to_broadcast([P, P]),
+                    rhs=ident[:],
+                    start=True,
+                    stop=True,
                 )
 
         def denominators(r):

@@ -69,10 +69,10 @@ def tile_pearsonattention_pa_t_kernel(tc, h, W_h, beta, out):
         nc.vector.tensor_copy(out=beta_f[:], in_=beta_bf[:])
 
         hT, h_grouped, h_q = {}, {}, {}
-        x, moments, negmean, xm = {}, {}, {}, {}
+        x, moments, neg_xm = {}, {}, {}
         rsqrt_sum, norm = {}, {}
         xT, x_grouped, x_q = {}, {}, {}
-        spread_cov, scale_abs = {}, {}
+        spread_cov, root_abs, scale_abs = {}, {}, {}
 
         def transpose_words(dst, src):
             for j in range(PAIR):
@@ -122,24 +122,20 @@ def tile_pearsonattention_pa_t_kernel(tc, h, W_h, beta, out):
         def statistics(r):
             parts = small.tile([P, PAIR, 6], F32, name="parts")
             moments[r] = small.tile([P, PAIR, 2], F32, name="moments")
-            negmean[r] = small.tile([P, PAIR], F32, name="negmean")
             for j in range(PAIR):
                 nc.vector.bn_stats(out=parts[:, j, :], in_=x[r][j][:])
             for j in range(PAIR):
                 nc.vector.bn_aggr(out=moments[r][:, j, :], in_=parts[:, j, :])
-            nc.vector.tensor_scalar(
-                out=negmean[r][:], in0=moments[r][:, :, 0], scalar1=-1.0, scalar2=None, op0=ALU.mult
-            )
 
         def subtract_mean(r):
-            xm[r] = work.tile([P, PAIR, F_OUT], BF16, name="xm")
+            neg_xm[r] = work.tile([P, PAIR, F_OUT], BF16, name="neg_xm")
             for j in range(PAIR):
                 nc.scalar.activation(
-                    out=xm[r][:, j, :],
+                    out=neg_xm[r][:, j, :],
                     in_=x[r][j][:],
                     func=ACT.Identity,
-                    bias=negmean[r][:, j : j + 1],
-                    scale=1.0,
+                    bias=moments[r][:, j, 0:1],
+                    scale=-1.0,
                 )
 
         def rsqrt_sums(r):
@@ -149,23 +145,18 @@ def tile_pearsonattention_pa_t_kernel(tc, h, W_h, beta, out):
                 in_=moments[r][:, :, 1],
                 func=ACT.Abs_reciprocal_sqrt,
                 bias=TINY,
-                scale=float(F_OUT),
+                scale=1.0 / F_OUT,
             )
 
         def norms(r):
             norm[r] = small.tile([P, PAIR], F32, name="norm")
-            nc.vector.scalar_tensor_tensor(
-                out=norm[r][:],
-                in0=moments[r][:, :, 1],
-                scalar=float(F_OUT),
-                in1=rsqrt_sum[r][:],
-                op0=ALU.mult,
-                op1=ALU.mult,
+            nc.gpsimd.tensor_tensor(
+                out=norm[r][:], in0=moments[r][:, :, 1], in1=rsqrt_sum[r][:], op=ALU.mult
             )
 
         def transpose_xm(r):
             xT[r] = psum.tile([P, PAIR, HALVES, P], F32, name="xT")
-            transpose_words(xT[r], xm[r])
+            transpose_words(xT[r], neg_xm[r])
 
         def copy_xT(r):
             x_grouped[r] = work.tile([P, PAIR, P, PACK], BF16, name="x_grouped", align_bytes=64)
@@ -189,18 +180,15 @@ def tile_pearsonattention_pa_t_kernel(tc, h, W_h, beta, out):
                     start=True,
                     stop=True,
                 )
+
+        def spread_norms(r):
             for j in range(PAIR):
-                nc.tensor.matmul(
-                    out=spread_cov[r][:, 0, j, :],
-                    lhsT=norm[r][:, j : j + 1].to_broadcast([P, P]),
-                    rhs=ident[:],
-                    start=True,
-                    stop=True,
+                nc.tensor.transpose(
+                    spread_cov[r][:, 0, j, :], norm[r][:, j : j + 1].to_broadcast([P, P]), ident[:]
                 )
 
         def denominators(r):
             root = work.tile([P, PAIR, P], F32, name="root")
-            inverse = work.tile([P, PAIR, P], F32, name="inverse")
             cov_abs = work.tile([P, PAIR, P], F32, name="cov_abs")
             for j in range(PAIR):
                 nc.scalar.activation(
@@ -211,7 +199,12 @@ def tile_pearsonattention_pa_t_kernel(tc, h, W_h, beta, out):
                     scale=norm[r][:, j : j + 1],
                 )
             nc.scalar.activation(out=cov_abs[:], in_=spread_cov[r][:, 1, :, :], func=ACT.Abs)
-            nc.scalar.activation(out=inverse[:], in_=root[:], func=ACT.Square)
+            root_abs[r] = (root, cov_abs)
+
+        def invert(r):
+            root, cov_abs = root_abs[r]
+            inverse = work.tile([P, PAIR, P], F32, name="inverse")
+            nc.gpsimd.tensor_tensor(out=inverse[:], in0=root[:], in1=root[:], op=ALU.mult)
             scale_abs[r] = (inverse, cov_abs)
 
         def scale_and_store(r):
@@ -232,20 +225,22 @@ def tile_pearsonattention_pa_t_kernel(tc, h, W_h, beta, out):
             if 0 <= r < N_PAIRS:
                 stage(r)
 
-        LAST_LAG = 4
+        LAST_LAG = 7
         for step in range(N_PAIRS + LAST_LAG):
             run(load_pair, step + LOAD_AHEAD)
-            run(correlate, step - 4)
-            run(transpose_xm, step - 3)
+            run(transpose_xm, step - 4)
+            run(quantise_h, step - 2)
+            run(project, step - 2)
+            run(correlate, step - 5)
             run(copy_hT, step - 1)
             run(transpose_h, step)
-            run(statistics, step - 2)
-            run(quantise_h, step - 1)
-            run(project, step - 1)
-            run(rsqrt_sums, step - 3)
-            run(denominators, step - 4)
-            run(subtract_mean, step - 2)
-            run(copy_xT, step - 3)
-            run(norms, step - 3)
+            run(spread_norms, step - 5)
+            run(statistics, step - 3)
+            run(rsqrt_sums, step - 4)
+            run(norms, step - 4)
+            run(denominators, step - 6)
+            run(invert, step - 6)
+            run(subtract_mean, step - 3)
+            run(copy_xT, step - 4)
             run(scale_and_store, step - LAST_LAG)
-            run(quantise_xm, step - 3)
+            run(quantise_xm, step - 4)

@@ -69,7 +69,7 @@ def tile_pearsonattention_pa_t_kernel(tc, h, W_h, beta, out):
         nc.vector.tensor_copy(out=beta_f[:], in_=beta_bf[:])
 
         hT, h_grouped, h_q = {}, {}, {}
-        x, moments, neg_xm = {}, {}, {}
+        x, parts, moments, neg_xm = {}, {}, {}, {}
         rsqrt_sum, norm = {}, {}
         xT, x_grouped, x_q = {}, {}, {}
         spread_cov, root_abs, scale_abs = {}, {}, {}
@@ -120,12 +120,16 @@ def tile_pearsonattention_pa_t_kernel(tc, h, W_h, beta, out):
                 x[r].append(x_j)
 
         def statistics(r):
-            parts = small.tile([P, PAIR, 6], F32, name="parts")
-            moments[r] = small.tile([P, PAIR, 2], F32, name="moments")
+            parts[r] = []
             for j in range(PAIR):
-                nc.vector.bn_stats(out=parts[:, j, :], in_=x[r][j][:])
-            for j in range(PAIR):
-                nc.vector.bn_aggr(out=moments[r][:, j, :], in_=parts[:, j, :])
+                parts_j = small.tile([P, 6], F32, name="parts", bufs=8 * PAIR)
+                nc.vector.bn_stats(out=parts_j[:], in_=x[r][j][:])
+                parts[r].append(parts_j)
+
+        def aggregate(r, j):
+            if j == 0:
+                moments[r] = small.tile([P, PAIR, 2], F32, name="moments")
+            nc.vector.bn_aggr(out=moments[r][:, j, :], in_=parts[r][j][:])
 
         def subtract_mean(r):
             neg_xm[r] = work.tile([P, PAIR, F_OUT], BF16, name="neg_xm")
@@ -221,9 +225,9 @@ def tile_pearsonattention_pa_t_kernel(tc, h, W_h, beta, out):
             graphs = slice(PAIR * r, PAIR * (r + 1))
             nc.sync.dma_start(out=out[graphs].rearrange("b n m -> n b m"), in_=result[:])
 
-        def run(stage, r):
+        def run(stage, r, *args):
             if 0 <= r < N_PAIRS:
-                stage(r)
+                stage(r, *args)
 
         LAST_LAG = 7
         for step in range(N_PAIRS + LAST_LAG):
@@ -236,11 +240,13 @@ def tile_pearsonattention_pa_t_kernel(tc, h, W_h, beta, out):
             run(transpose_h, step)
             run(spread_norms, step - 5)
             run(statistics, step - 3)
+            run(aggregate, step - 3, 0)
+            run(copy_xT, step - 4)
+            run(aggregate, step - 3, 1)
             run(rsqrt_sums, step - 4)
             run(norms, step - 4)
             run(denominators, step - 6)
             run(invert, step - 6)
             run(subtract_mean, step - 3)
-            run(copy_xT, step - 4)
             run(scale_and_store, step - LAST_LAG)
             run(quantise_xm, step - 4)

@@ -19,6 +19,10 @@ PACK = 4
 HALVES = 2
 PAIR = 2
 N_PAIRS = GRAPHS // PAIR
+H_CALL = 2
+X_CALL = 6
+V_NODES = slice(0, 192)
+S_NODES = slice(192, 256)
 LOAD_AHEAD = 4
 EPS = 1e-8
 TINY = 1e-30
@@ -30,7 +34,7 @@ def tile_pearsonattention_pa_t_kernel(tc, h, W_h, beta, out):
     nc = tc.nc
     with ExitStack() as ctx:
         keep = ctx.enter_context(tc.tile_pool(name="keep", bufs=1))
-        work = ctx.enter_context(tc.tile_pool(name="work", bufs=3))
+        work = ctx.enter_context(tc.tile_pool(name="work", bufs=4))
         small = ctx.enter_context(tc.tile_pool(name="small", bufs=8))
         psum = ctx.enter_context(tc.psum_pool(name="psum", bufs=1))
         ctx.enter_context(tc.manual_schedule())
@@ -43,15 +47,19 @@ def tile_pearsonattention_pa_t_kernel(tc, h, W_h, beta, out):
             graphs = slice(PAIR * r, PAIR * (r + 1))
             nc.sync.dma_start(out=h_all[:, graphs, :], in_=h[graphs].rearrange("b n k -> n b k"))
 
-        load_pair(0)
         for u in range(HALVES):
             rows = W_h[256 * u : 256 * (u + 1), :]
             nc.sync.dma_start(
                 out=w_raw[:, 2 * u : 2 * u + 2, :], in_=rows.rearrange("(p e) c -> p e c", e=2)
             )
-        for r in range(1, LOAD_AHEAD):
+        for r in range(LOAD_AHEAD):
             load_pair(r)
         nc.sync.dma_start(out=beta_bf[:], in_=beta.partition_broadcast(P))
+
+        one = keep.tile([P, 1], F32)
+        warm = keep.tile([P, 1], F32)
+        nc.vector.memset(one[:], 1.0)
+        nc.scalar.activation(out=warm[:], in_=one[:], func=ACT.Abs_reciprocal_sqrt)
 
         ident = keep.tile([P, P], F32)
         make_identity(nc, ident[:])
@@ -68,50 +76,58 @@ def tile_pearsonattention_pa_t_kernel(tc, h, W_h, beta, out):
         beta_f = keep.tile([P, 1], F32)
         nc.vector.tensor_copy(out=beta_f[:], in_=beta_bf[:])
 
-        hT, h_grouped, h_q = {}, {}, {}
+        hT, grouped, quantised = {}, {}, {}
         x, parts, moments, neg_xm = {}, {}, {}, {}
         rsqrt_sum, norm = {}, {}
-        xT, x_grouped, x_q = {}, {}, {}
-        spread_cov, root_abs, scale_abs = {}, {}, {}
+        xT, spread_cov, root_abs, scale_abs = {}, {}, {}, {}
 
         def transpose_words(dst, src):
             for j in range(PAIR):
                 words = src[:, j, :].bitcast(F32)
                 for u in range(HALVES):
-                    nc.tensor.transpose(dst[:, j, u, :], words[:, P * u : P * (u + 1)], ident[:])
+                    nc.tensor.transpose(dst[:, u, j, :], words[:, P * u : P * (u + 1)], ident[:])
 
-        def quantise(grouped, name):
-            codes = work.tile([P, PAIR, P], U32, name=name + "_codes", align_bytes=64)
-            scales = work.tile([P, PAIR, P], U8, name=name + "_scales", align_bytes=64)
+        def grouped_of(q):
+            if q not in grouped:
+                grouped[q] = work.tile([P, 2, PAIR * P, PACK], BF16, name="grouped", align_bytes=64)
+            return grouped[q]
+
+        def quantise(q):
+            codes = work.tile([P, 2, PAIR * P], U32, name="codes", align_bytes=64)
+            scales = work.tile([P, 2, PAIR * P], U8, name="scales", align_bytes=64)
+            lo = 0 if q - H_CALL < N_PAIRS else 1
+            hi = 2 if q - X_CALL >= 0 else 1
             nc.vector.quantize_mx(
-                out=codes[:].rearrange("p j n -> p (j n)").bitcast(FP8X4),
-                scales=scales[:].rearrange("p j n -> p (j n)"),
-                in_=grouped[:].rearrange("p j n t -> p (j n t)"),
+                out=codes[:, lo:hi, :].rearrange("p s c -> p (s c)").bitcast(FP8X4),
+                scales=scales[:, lo:hi, :].rearrange("p s c -> p (s c)"),
+                in_=grouped[q][:, lo:hi, :, :].rearrange("p s c t -> p (s c t)"),
             )
-            return codes, scales
+            quantised[q] = (codes, scales)
+
+        def operand(q, s, j):
+            codes, scales = quantised[q]
+            nodes = slice(P * j, P * (j + 1))
+            return codes[:, s, nodes].bitcast(FP8X4), scales[:, s, nodes]
 
         def transpose_h(r):
-            hT[r] = psum.tile([P, PAIR, HALVES, P], F32, name="hT")
+            hT[r] = psum.tile([P, HALVES, PAIR, P], F32, name="hT")
             transpose_words(hT[r], h_all[:, PAIR * r : PAIR * (r + 1), :])
 
         def copy_hT(r):
-            h_grouped[r] = work.tile([P, PAIR, P, PACK], BF16, name="h_grouped", align_bytes=64)
             nc.scalar.copy(
-                out=h_grouped[r][:].bitcast(F32), in_=hT[r][:].rearrange("p j u n -> p j n u")
+                out=grouped_of(r + H_CALL)[:, 0, :, :].bitcast(F32),
+                in_=hT[r][:].rearrange("p u j n -> p (j n) u"),
             )
 
-        def quantise_h(r):
-            h_q[r] = quantise(h_grouped[r], "h")
-
         def project(r):
-            codes, scales = h_q[r]
             x[r] = []
             for j in range(PAIR):
+                h_codes, h_scales = operand(r + H_CALL, 0, j)
                 x_j = psum.tile([P, F_OUT], F32, name="x", bufs=2 * PAIR)
                 nc.tensor.matmul_mx(
                     out=x_j[:],
-                    lhsT=codes[:, j, :].bitcast(FP8X4),
-                    lhsT_scale=scales[:, j, :],
+                    lhsT=h_codes,
+                    lhsT_scale=h_scales,
                     rhs=w_codes[:].bitcast(FP8X4),
                     rhs_scale=w_scales[:],
                     start=True,
@@ -131,16 +147,16 @@ def tile_pearsonattention_pa_t_kernel(tc, h, W_h, beta, out):
                 moments[r] = small.tile([P, PAIR, 2], F32, name="moments")
             nc.vector.bn_aggr(out=moments[r][:, j, :], in_=parts[r][j][:])
 
-        def subtract_mean(r):
-            neg_xm[r] = work.tile([P, PAIR, F_OUT], BF16, name="neg_xm")
-            for j in range(PAIR):
-                nc.scalar.activation(
-                    out=neg_xm[r][:, j, :],
-                    in_=x[r][j][:],
-                    func=ACT.Identity,
-                    bias=moments[r][:, j, 0:1],
-                    scale=-1.0,
-                )
+        def subtract_mean(r, j):
+            if j == 0:
+                neg_xm[r] = work.tile([P, PAIR, F_OUT], BF16, name="neg_xm")
+            nc.scalar.activation(
+                out=neg_xm[r][:, j, :],
+                in_=x[r][j][:],
+                func=ACT.Identity,
+                bias=moments[r][:, j, 0:1],
+                scale=-1.0,
+            )
 
         def rsqrt_sums(r):
             rsqrt_sum[r] = small.tile([P, PAIR], F32, name="rsqrt_sum")
@@ -159,33 +175,30 @@ def tile_pearsonattention_pa_t_kernel(tc, h, W_h, beta, out):
             )
 
         def transpose_xm(r):
-            xT[r] = psum.tile([P, PAIR, HALVES, P], F32, name="xT")
+            xT[r] = psum.tile([P, HALVES, PAIR, P], F32, name="xT")
             transpose_words(xT[r], neg_xm[r])
 
-        def copy_xT(r):
-            x_grouped[r] = work.tile([P, PAIR, P, PACK], BF16, name="x_grouped", align_bytes=64)
-            nc.vector.tensor_copy(
-                out=x_grouped[r][:].bitcast(F32), in_=xT[r][:].rearrange("p j u n -> p j n u")
+        def copy_xT(r, copy, nodes):
+            copy(
+                out=grouped_of(r + X_CALL)[:, 1, nodes, :].bitcast(F32),
+                in_=xT[r][:].rearrange("p u j n -> p (j n) u")[:, nodes, :],
             )
 
-        def quantise_xm(r):
-            x_q[r] = quantise(x_grouped[r], "x")
-
         def correlate(r):
-            codes, scales = x_q[r]
-            spread_cov[r] = psum.tile([P, 2, PAIR, P], F32, name="spread_cov", bufs=2)
             for j in range(PAIR):
+                x_codes, x_scales = operand(r + X_CALL, 1, j)
                 nc.tensor.matmul_mx(
                     out=spread_cov[r][:, 1, j, :],
-                    lhsT=codes[:, j, :].bitcast(FP8X4),
-                    lhsT_scale=scales[:, j, :],
-                    rhs=codes[:, j, :].bitcast(FP8X4),
-                    rhs_scale=scales[:, j, :],
+                    lhsT=x_codes,
+                    lhsT_scale=x_scales,
+                    rhs=x_codes,
+                    rhs_scale=x_scales,
                     start=True,
                     stop=True,
                 )
 
         def spread_norms(r):
+            spread_cov[r] = psum.tile([P, 2, PAIR, P], F32, name="spread_cov", bufs=2)
             for j in range(PAIR):
                 nc.tensor.transpose(
                     spread_cov[r][:, 0, j, :], norm[r][:, j : j + 1].to_broadcast([P, P]), ident[:]
@@ -229,24 +242,26 @@ def tile_pearsonattention_pa_t_kernel(tc, h, W_h, beta, out):
             if 0 <= r < N_PAIRS:
                 stage(r, *args)
 
-        LAST_LAG = 7
+        LAST_LAG = 8
         for step in range(N_PAIRS + LAST_LAG):
             run(load_pair, step + LOAD_AHEAD)
+            if step >= H_CALL and step - X_CALL < N_PAIRS:
+                quantise(step)
             run(transpose_xm, step - 4)
-            run(quantise_h, step - 2)
             run(project, step - 2)
-            run(correlate, step - 5)
+            run(correlate, step - 6)
             run(copy_hT, step - 1)
             run(transpose_h, step)
             run(spread_norms, step - 5)
+            run(scale_and_store, step - LAST_LAG)
             run(statistics, step - 3)
             run(aggregate, step - 3, 0)
-            run(copy_xT, step - 4)
+            run(subtract_mean, step - 3, 0)
+            run(copy_xT, step - 4, nc.vector.tensor_copy, V_NODES)
+            run(copy_xT, step - 4, nc.scalar.copy, S_NODES)
             run(aggregate, step - 3, 1)
-            run(rsqrt_sums, step - 4)
-            run(norms, step - 4)
+            run(subtract_mean, step - 3, 1)
+            run(rsqrt_sums, step - 3)
+            run(norms, step - 3)
             run(denominators, step - 6)
             run(invert, step - 6)
-            run(subtract_mean, step - 3)
-            run(scale_and_store, step - LAST_LAG)
-            run(quantise_xm, step - 4)

@@ -18,11 +18,12 @@ F_OUT = 512
 PACK = 4
 HALVES = 2
 PAIR = 2
+BOTH = (0, 1)
 N_PAIRS = GRAPHS // PAIR
 H_CALL = 2
 X_CALL = 6
-V_NODES = slice(0, 192)
-S_NODES = slice(192, 256)
+V_NODES = slice(0, 176)
+S_NODES = slice(176, 256)
 LOAD_AHEAD = 4
 EPS = 1e-8
 TINY = 1e-30
@@ -42,6 +43,7 @@ def tile_pearsonattention_pa_t_kernel(tc, h, W_h, beta, out):
         h_all = keep.tile([P, GRAPHS, F_IN], BF16)
         w_raw = keep.tile([P, PACK, F_OUT], BF16)
         beta_bf = keep.tile([P, 1], BF16)
+        result = keep.tile([P, GRAPHS, P], F32)
 
         def load_pair(r):
             graphs = slice(PAIR * r, PAIR * (r + 1))
@@ -79,10 +81,10 @@ def tile_pearsonattention_pa_t_kernel(tc, h, W_h, beta, out):
         hT, grouped, quantised = {}, {}, {}
         x, parts, moments, neg_xm = {}, {}, {}, {}
         rsqrt_sum, norm = {}, {}
-        xT, spread_cov, root_abs, scale_abs = {}, {}, {}, {}
+        xT, spread_cov, root, inverse, cov_abs = {}, {}, {}, {}, {}
 
-        def transpose_words(dst, src):
-            for j in range(PAIR):
+        def transpose_words(dst, src, js):
+            for j in js:
                 words = src[:, j, :].bitcast(F32)
                 for u in range(HALVES):
                     nc.tensor.transpose(dst[:, u, j, :], words[:, P * u : P * (u + 1)], ident[:])
@@ -92,17 +94,19 @@ def tile_pearsonattention_pa_t_kernel(tc, h, W_h, beta, out):
                 grouped[q] = work.tile([P, 2, PAIR * P, PACK], BF16, name="grouped", align_bytes=64)
             return grouped[q]
 
-        def quantise(q):
-            codes = work.tile([P, 2, PAIR * P], U32, name="codes", align_bytes=64)
-            scales = work.tile([P, 2, PAIR * P], U8, name="scales", align_bytes=64)
+        def quantise(q, columns=slice(0, PAIR * P)):
+            if q not in quantised:
+                codes = work.tile([P, 2, PAIR * P], U32, name="codes", align_bytes=64)
+                scales = work.tile([P, 2, PAIR * P], U8, name="scales", align_bytes=64)
+                quantised[q] = (codes, scales)
+            codes, scales = quantised[q]
             lo = 0 if q - H_CALL < N_PAIRS else 1
             hi = 2 if q - X_CALL >= 0 else 1
             nc.vector.quantize_mx(
-                out=codes[:, lo:hi, :].rearrange("p s c -> p (s c)").bitcast(FP8X4),
-                scales=scales[:, lo:hi, :].rearrange("p s c -> p (s c)"),
-                in_=grouped[q][:, lo:hi, :, :].rearrange("p s c t -> p (s c t)"),
+                out=codes[:, lo:hi, columns].rearrange("p s c -> p (s c)").bitcast(FP8X4),
+                scales=scales[:, lo:hi, columns].rearrange("p s c -> p (s c)"),
+                in_=grouped[q][:, lo:hi, columns, :].rearrange("p s c t -> p (s c t)"),
             )
-            quantised[q] = (codes, scales)
 
         def operand(q, s, j):
             codes, scales = quantised[q]
@@ -110,8 +114,8 @@ def tile_pearsonattention_pa_t_kernel(tc, h, W_h, beta, out):
             return codes[:, s, nodes].bitcast(FP8X4), scales[:, s, nodes]
 
         def transpose_h(r):
-            hT[r] = psum.tile([P, HALVES, PAIR, P], F32, name="hT")
-            transpose_words(hT[r], h_all[:, PAIR * r : PAIR * (r + 1), :])
+            hT[r] = psum.tile([P, HALVES, PAIR, P], F32, name="words", bufs=2)
+            transpose_words(hT[r], h_all[:, PAIR * r : PAIR * (r + 1), :], BOTH)
 
         def copy_hT(r):
             nc.scalar.copy(
@@ -135,17 +139,14 @@ def tile_pearsonattention_pa_t_kernel(tc, h, W_h, beta, out):
                 )
                 x[r].append(x_j)
 
-        def statistics(r):
-            parts[r] = []
-            for j in range(PAIR):
-                parts_j = small.tile([P, 6], F32, name="parts", bufs=8 * PAIR)
-                nc.vector.bn_stats(out=parts_j[:], in_=x[r][j][:])
-                parts[r].append(parts_j)
+        def statistics(r, j):
+            parts[r, j] = small.tile([P, 6], F32, name="parts", bufs=8 * PAIR)
+            nc.vector.bn_stats(out=parts[r, j][:], in_=x[r][j][:])
 
         def aggregate(r, j):
             if j == 0:
                 moments[r] = small.tile([P, PAIR, 2], F32, name="moments")
-            nc.vector.bn_aggr(out=moments[r][:, j, :], in_=parts[r][j][:])
+            nc.vector.bn_aggr(out=moments[r][:, j, :], in_=parts[r, j][:])
 
         def subtract_mean(r, j):
             if j == 0:
@@ -174,18 +175,21 @@ def tile_pearsonattention_pa_t_kernel(tc, h, W_h, beta, out):
                 out=norm[r][:], in0=moments[r][:, :, 1], in1=rsqrt_sum[r][:], op=ALU.mult
             )
 
-        def transpose_xm(r):
-            xT[r] = psum.tile([P, HALVES, PAIR, P], F32, name="xT")
-            transpose_words(xT[r], neg_xm[r])
+        def transpose_xm(r, js=BOTH):
+            words = psum.tile([P, HALVES, PAIR, P], F32, name="words", bufs=2)
+            transpose_words(words, neg_xm[r], js)
+            for j in js:
+                xT[r, j] = words
 
         def copy_xT(r, copy, nodes):
+            words = xT[r, nodes.start // P]
             copy(
                 out=grouped_of(r + X_CALL)[:, 1, nodes, :].bitcast(F32),
-                in_=xT[r][:].rearrange("p u j n -> p (j n) u")[:, nodes, :],
+                in_=words[:].rearrange("p u j n -> p (j n) u")[:, nodes, :],
             )
 
-        def correlate(r):
-            for j in range(PAIR):
+        def correlate(r, js=BOTH):
+            for j in js:
                 x_codes, x_scales = operand(r + X_CALL, 1, j)
                 nc.tensor.matmul_mx(
                     out=spread_cov[r][:, 1, j, :],
@@ -204,64 +208,119 @@ def tile_pearsonattention_pa_t_kernel(tc, h, W_h, beta, out):
                     spread_cov[r][:, 0, j, :], norm[r][:, j : j + 1].to_broadcast([P, P]), ident[:]
                 )
 
-        def denominators(r):
-            root = work.tile([P, PAIR, P], F32, name="root")
-            cov_abs = work.tile([P, PAIR, P], F32, name="cov_abs")
+        def roots(r):
+            root[r] = work.tile([P, PAIR, P], F32, name="root")
             for j in range(PAIR):
                 nc.scalar.activation(
-                    out=root[:, j, :],
+                    out=root[r][:, j, :],
                     in_=spread_cov[r][:, 0, j, :],
                     func=ACT.Abs_reciprocal_sqrt,
                     bias=EPS,
                     scale=norm[r][:, j : j + 1],
                 )
-            nc.scalar.activation(out=cov_abs[:], in_=spread_cov[r][:, 1, :, :], func=ACT.Abs)
-            root_abs[r] = (root, cov_abs)
 
-        def invert(r):
-            root, cov_abs = root_abs[r]
-            inverse = work.tile([P, PAIR, P], F32, name="inverse")
-            nc.gpsimd.tensor_tensor(out=inverse[:], in0=root[:], in1=root[:], op=ALU.mult)
-            scale_abs[r] = (inverse, cov_abs)
+        def invert(r, engine):
+            inverse[r] = work.tile([P, PAIR, P], F32, name="inverse")
+            engine.tensor_tensor(out=inverse[r][:], in0=root[r][:], in1=root[r][:], op=ALU.mult)
 
-        def scale_and_store(r):
-            inverse, cov_abs = scale_abs[r]
-            result = work.tile([P, PAIR, P], F32, name="result")
+        def magnitudes(r, js=BOTH):
+            if r not in cov_abs:
+                cov_abs[r] = work.tile([P, PAIR, P], F32, name="cov_abs")
+            js = slice(js[0], js[-1] + 1)
+            nc.scalar.activation(
+                out=cov_abs[r][:, js, :], in_=spread_cov[r][:, 1, js, :], func=ACT.Abs
+            )
+
+        def scale_and_store(r, js=BOTH):
+            graphs = slice(PAIR * r + js[0], PAIR * r + js[-1] + 1)
+            js = slice(js[0], js[-1] + 1)
             nc.vector.scalar_tensor_tensor(
-                out=result[:].rearrange("p j m -> p (j m)"),
-                in0=cov_abs[:].rearrange("p j m -> p (j m)"),
+                out=result[:, graphs, :].rearrange("p j m -> p (j m)"),
+                in0=cov_abs[r][:, js, :].rearrange("p j m -> p (j m)"),
                 scalar=beta_f[:, 0:1],
-                in1=inverse[:].rearrange("p j m -> p (j m)"),
+                in1=inverse[r][:, js, :].rearrange("p j m -> p (j m)"),
                 op0=ALU.mult,
                 op1=ALU.mult,
             )
-            graphs = slice(PAIR * r, PAIR * (r + 1))
-            nc.sync.dma_start(out=out[graphs].rearrange("b n m -> n b m"), in_=result[:])
+            nc.sync.dma_start(out=out[graphs].rearrange("b n m -> n b m"), in_=result[:, graphs, :])
 
         def run(stage, r, *args):
             if 0 <= r < N_PAIRS:
                 stage(r, *args)
 
         LAST_LAG = 8
-        for step in range(N_PAIRS + LAST_LAG):
+        for step in range(N_PAIRS + 2):
             run(load_pair, step + LOAD_AHEAD)
-            if step >= H_CALL and step - X_CALL < N_PAIRS:
+            if step >= H_CALL:
                 quantise(step)
             run(transpose_xm, step - 4)
             run(project, step - 2)
+            run(roots, step - 6)
             run(correlate, step - 6)
             run(copy_hT, step - 1)
             run(transpose_h, step)
             run(spread_norms, step - 5)
-            run(scale_and_store, step - LAST_LAG)
-            run(statistics, step - 3)
+            run(statistics, step - 3, 0)
+            run(statistics, step - 3, 1)
             run(aggregate, step - 3, 0)
             run(subtract_mean, step - 3, 0)
             run(copy_xT, step - 4, nc.vector.tensor_copy, V_NODES)
             run(copy_xT, step - 4, nc.scalar.copy, S_NODES)
             run(aggregate, step - 3, 1)
             run(subtract_mean, step - 3, 1)
+            run(scale_and_store, step - LAST_LAG)
             run(rsqrt_sums, step - 3)
             run(norms, step - 3)
-            run(denominators, step - 6)
-            run(invert, step - 6)
+            run(invert, step - 6, nc.gpsimd)
+            run(magnitudes, step - 6)
+
+        d = N_PAIRS - 1
+        a, b, c = d - 3, d - 2, d - 1
+        nodes = [slice(P * j, P * (j + 1)) for j in range(PAIR)]
+        quantise(a + X_CALL)
+        transpose_xm(c)
+        spread_norms(b)
+        roots(a)
+        correlate(a)
+        statistics(d, 0)
+        scale_and_store(a - 2)
+        aggregate(d, 0)
+        statistics(d, 1)
+        quantise(b + X_CALL)
+        aggregate(d, 1)
+        subtract_mean(d, 0)
+        magnitudes(a)
+        roots(b)
+        correlate(b)
+        scale_and_store(a - 1)
+        invert(a, nc.vector)
+        subtract_mean(d, 1)
+        rsqrt_sums(d)
+        norms(d)
+        copy_xT(c, nc.vector.tensor_copy, slice(0, PAIR * P))
+        transpose_xm(d, [0])
+        spread_norms(c)
+        magnitudes(b)
+        scale_and_store(a)
+        quantise(c + X_CALL)
+        roots(c)
+        copy_xT(d, nc.vector.tensor_copy, nodes[0])
+        transpose_xm(d, [1])
+        invert(b, nc.gpsimd)
+        copy_xT(d, nc.scalar.copy, nodes[1])
+        spread_norms(d)
+        correlate(c)
+        roots(d)
+        quantise(d + X_CALL, nodes[0])
+        quantise(d + X_CALL, nodes[1])
+        magnitudes(c)
+        scale_and_store(b)
+        invert(c, nc.vector)
+        invert(d, nc.vector)
+        correlate(d, [0])
+        correlate(d, [1])
+        magnitudes(d, [0])
+        magnitudes(d, [1])
+        scale_and_store(c)
+        scale_and_store(d, [0])
+        scale_and_store(d, [1])

from contextlib import ExitStack

import concourse.mybir as mybir
from concourse.masks import make_identity

F32 = mybir.dt.float32
BF16 = mybir.dt.bfloat16
U32 = mybir.dt.uint32
U8 = mybir.dt.uint8
FP8X4 = mybir.dt.float8_e4m3fn_x4
ACT = mybir.ActivationFunctionType
ALU = mybir.AluOpType

GRAPHS = 64
P = 128
F_IN = 512
F_OUT = 512
PACK = 4
HALVES = 2
PAIR = 2
BOTH = (0, 1)
N_PAIRS = GRAPHS // PAIR
H_CALL = 2
X_CALL = 6
V_NODES = slice(0, 176)
S_NODES = slice(176, 256)
LOAD_AHEAD = 4
EPS = 1e-8
TINY = 1e-30

FLOPS = 2 * GRAPHS * P * F_IN * F_OUT + 2 * GRAPHS * P * P * F_OUT


def tile_pearsonattention_pa_t_kernel(tc, h, W_h, beta, out):
    nc = tc.nc
    with ExitStack() as ctx:
        keep = ctx.enter_context(tc.tile_pool(name="keep", bufs=1))
        work = ctx.enter_context(tc.tile_pool(name="work", bufs=4))
        small = ctx.enter_context(tc.tile_pool(name="small", bufs=8))
        psum = ctx.enter_context(tc.psum_pool(name="psum", bufs=1))
        ctx.enter_context(tc.manual_schedule())

        h_all = keep.tile([P, GRAPHS, F_IN], BF16)
        w_raw = keep.tile([P, PACK, F_OUT], BF16)
        beta_bf = keep.tile([P, 1], BF16)
        result = keep.tile([P, GRAPHS, P], F32)

        def load_pair(r):
            graphs = slice(PAIR * r, PAIR * (r + 1))
            nc.sync.dma_start(out=h_all[:, graphs, :], in_=h[graphs].rearrange("b n k -> n b k"))

        for u in range(HALVES):
            rows = W_h[256 * u : 256 * (u + 1), :]
            nc.sync.dma_start(
                out=w_raw[:, 2 * u : 2 * u + 2, :], in_=rows.rearrange("(p e) c -> p e c", e=2)
            )
        for r in range(LOAD_AHEAD):
            load_pair(r)
        nc.sync.dma_start(out=beta_bf[:], in_=beta.partition_broadcast(P))

        one = keep.tile([P, 1], F32)
        warm = keep.tile([P, 1], F32)
        nc.vector.memset(one[:], 1.0)
        nc.scalar.activation(out=warm[:], in_=one[:], func=ACT.Abs_reciprocal_sqrt)

        ident = keep.tile([P, P], F32)
        make_identity(nc, ident[:])

        w_grouped = keep.tile([P, F_OUT, PACK], BF16, align_bytes=64)
        w_codes = keep.tile([P, F_OUT], U32, align_bytes=64)
        w_scales = keep.tile([P, F_OUT], U8, align_bytes=64)
        nc.vector.tensor_copy(out=w_grouped[:], in_=w_raw[:].rearrange("p t c -> p c t"))
        nc.vector.quantize_mx(
            out=w_codes[:].bitcast(FP8X4),
            scales=w_scales[:],
            in_=w_grouped[:].rearrange("p c t -> p (c t)"),
        )
        beta_f = keep.tile([P, 1], F32)
        nc.vector.tensor_copy(out=beta_f[:], in_=beta_bf[:])

        hT, grouped, quantised = {}, {}, {}
        x, parts, moments, neg_xm = {}, {}, {}, {}
        rsqrt_sum, norm = {}, {}
        xT, spread_cov, root, inverse, cov_abs = {}, {}, {}, {}, {}

        def transpose_words(dst, src, js):
            for j in js:
                words = src[:, j, :].bitcast(F32)
                for u in range(HALVES):
                    nc.tensor.transpose(dst[:, u, j, :], words[:, P * u : P * (u + 1)], ident[:])

        def grouped_of(q):
            if q not in grouped:
                grouped[q] = work.tile([P, 2, PAIR * P, PACK], BF16, name="grouped", align_bytes=64)
            return grouped[q]

        def quantise(q, columns=slice(0, PAIR * P)):
            if q not in quantised:
                codes = work.tile([P, 2, PAIR * P], U32, name="codes", align_bytes=64)
                scales = work.tile([P, 2, PAIR * P], U8, name="scales", align_bytes=64)
                quantised[q] = (codes, scales)
            codes, scales = quantised[q]
            lo = 0 if q - H_CALL < N_PAIRS else 1
            hi = 2 if q - X_CALL >= 0 else 1
            nc.vector.quantize_mx(
                out=codes[:, lo:hi, columns].rearrange("p s c -> p (s c)").bitcast(FP8X4),
                scales=scales[:, lo:hi, columns].rearrange("p s c -> p (s c)"),
                in_=grouped[q][:, lo:hi, columns, :].rearrange("p s c t -> p (s c t)"),
            )

        def operand(q, s, j):
            codes, scales = quantised[q]
            nodes = slice(P * j, P * (j + 1))
            return codes[:, s, nodes].bitcast(FP8X4), scales[:, s, nodes]

        def transpose_h(r):
            hT[r] = psum.tile([P, HALVES, PAIR, P], F32, name="words", bufs=2)
            transpose_words(hT[r], h_all[:, PAIR * r : PAIR * (r + 1), :], BOTH)

        def copy_hT(r):
            nc.scalar.copy(
                out=grouped_of(r + H_CALL)[:, 0, :, :].bitcast(F32),
                in_=hT[r][:].rearrange("p u j n -> p (j n) u"),
            )

        def project(r):
            x[r] = []
            for j in range(PAIR):
                h_codes, h_scales = operand(r + H_CALL, 0, j)
                x_j = psum.tile([P, F_OUT], F32, name="x", bufs=2 * PAIR)
                nc.tensor.matmul_mx(
                    out=x_j[:],
                    lhsT=h_codes,
                    lhsT_scale=h_scales,
                    rhs=w_codes[:].bitcast(FP8X4),
                    rhs_scale=w_scales[:],
                    start=True,
                    stop=True,
                )
                x[r].append(x_j)

        def statistics(r, j):
            parts[r, j] = small.tile([P, 6], F32, name="parts", bufs=8 * PAIR)
            nc.vector.bn_stats(out=parts[r, j][:], in_=x[r][j][:])

        def aggregate(r, j):
            if j == 0:
                moments[r] = small.tile([P, PAIR, 2], F32, name="moments")
            nc.vector.bn_aggr(out=moments[r][:, j, :], in_=parts[r, j][:])

        def subtract_mean(r, j):
            if j == 0:
                neg_xm[r] = work.tile([P, PAIR, F_OUT], BF16, name="neg_xm")
            nc.scalar.activation(
                out=neg_xm[r][:, j, :],
                in_=x[r][j][:],
                func=ACT.Identity,
                bias=moments[r][:, j, 0:1],
                scale=-1.0,
            )

        def rsqrt_sums(r):
            rsqrt_sum[r] = small.tile([P, PAIR], F32, name="rsqrt_sum")
            nc.scalar.activation(
                out=rsqrt_sum[r][:],
                in_=moments[r][:, :, 1],
                func=ACT.Abs_reciprocal_sqrt,
                bias=TINY,
                scale=1.0 / F_OUT,
            )

        def norms(r):
            norm[r] = small.tile([P, PAIR], F32, name="norm")
            nc.gpsimd.tensor_tensor(
                out=norm[r][:], in0=moments[r][:, :, 1], in1=rsqrt_sum[r][:], op=ALU.mult
            )

        def transpose_xm(r, js=BOTH):
            words = psum.tile([P, HALVES, PAIR, P], F32, name="words", bufs=2)
            transpose_words(words, neg_xm[r], js)
            for j in js:
                xT[r, j] = words

        def copy_xT(r, copy, nodes):
            words = xT[r, nodes.start // P]
            copy(
                out=grouped_of(r + X_CALL)[:, 1, nodes, :].bitcast(F32),
                in_=words[:].rearrange("p u j n -> p (j n) u")[:, nodes, :],
            )

        def correlate(r, js=BOTH):
            for j in js:
                x_codes, x_scales = operand(r + X_CALL, 1, j)
                nc.tensor.matmul_mx(
                    out=spread_cov[r][:, 1, j, :],
                    lhsT=x_codes,
                    lhsT_scale=x_scales,
                    rhs=x_codes,
                    rhs_scale=x_scales,
                    start=True,
                    stop=True,
                )

        def spread_norms(r):
            spread_cov[r] = psum.tile([P, 2, PAIR, P], F32, name="spread_cov", bufs=2)
            for j in range(PAIR):
                nc.tensor.transpose(
                    spread_cov[r][:, 0, j, :], norm[r][:, j : j + 1].to_broadcast([P, P]), ident[:]
                )

        def roots(r):
            root[r] = work.tile([P, PAIR, P], F32, name="root")
            for j in range(PAIR):
                nc.scalar.activation(
                    out=root[r][:, j, :],
                    in_=spread_cov[r][:, 0, j, :],
                    func=ACT.Abs_reciprocal_sqrt,
                    bias=EPS,
                    scale=norm[r][:, j : j + 1],
                )

        def invert(r, engine):
            inverse[r] = work.tile([P, PAIR, P], F32, name="inverse")
            engine.tensor_tensor(out=inverse[r][:], in0=root[r][:], in1=root[r][:], op=ALU.mult)

        def magnitudes(r, js=BOTH):
            if r not in cov_abs:
                cov_abs[r] = work.tile([P, PAIR, P], F32, name="cov_abs")
            js = slice(js[0], js[-1] + 1)
            nc.scalar.activation(
                out=cov_abs[r][:, js, :], in_=spread_cov[r][:, 1, js, :], func=ACT.Abs
            )

        def scale_and_store(r, js=BOTH):
            graphs = slice(PAIR * r + js[0], PAIR * r + js[-1] + 1)
            js = slice(js[0], js[-1] + 1)
            nc.vector.scalar_tensor_tensor(
                out=result[:, graphs, :].rearrange("p j m -> p (j m)"),
                in0=cov_abs[r][:, js, :].rearrange("p j m -> p (j m)"),
                scalar=beta_f[:, 0:1],
                in1=inverse[r][:, js, :].rearrange("p j m -> p (j m)"),
                op0=ALU.mult,
                op1=ALU.mult,
            )
            nc.sync.dma_start(out=out[graphs].rearrange("b n m -> n b m"), in_=result[:, graphs, :])

        def run(stage, r, *args):
            if 0 <= r < N_PAIRS:
                stage(r, *args)

        LAST_LAG = 8
        for step in range(N_PAIRS + 2):
            run(load_pair, step + LOAD_AHEAD)
            if step >= H_CALL:
                quantise(step)
            run(transpose_xm, step - 4)
            run(project, step - 2)
            run(roots, step - 6)
            run(correlate, step - 6)
            run(copy_hT, step - 1)
            run(transpose_h, step)
            run(spread_norms, step - 5)
            run(statistics, step - 3, 0)
            run(statistics, step - 3, 1)
            run(aggregate, step - 3, 0)
            run(subtract_mean, step - 3, 0)
            run(copy_xT, step - 4, nc.vector.tensor_copy, V_NODES)
            run(copy_xT, step - 4, nc.scalar.copy, S_NODES)
            run(aggregate, step - 3, 1)
            run(subtract_mean, step - 3, 1)
            run(scale_and_store, step - LAST_LAG)
            run(rsqrt_sums, step - 3)
            run(norms, step - 3)
            run(invert, step - 6, nc.gpsimd)
            run(magnitudes, step - 6)

        d = N_PAIRS - 1
        a, b, c = d - 3, d - 2, d - 1
        nodes = [slice(P * j, P * (j + 1)) for j in range(PAIR)]
        quantise(a + X_CALL)
        transpose_xm(c)
        spread_norms(b)
        roots(a)
        correlate(a)
        statistics(d, 0)
        scale_and_store(a - 2)
        aggregate(d, 0)
        statistics(d, 1)
        quantise(b + X_CALL)
        aggregate(d, 1)
        subtract_mean(d, 0)
        magnitudes(a)
        roots(b)
        correlate(b)
        scale_and_store(a - 1)
        invert(a, nc.vector)
        subtract_mean(d, 1)
        rsqrt_sums(d)
        norms(d)
        copy_xT(c, nc.vector.tensor_copy, slice(0, PAIR * P))
        transpose_xm(d, [0])
        spread_norms(c)
        magnitudes(b)
        scale_and_store(a)
        quantise(c + X_CALL)
        roots(c)
        copy_xT(d, nc.vector.tensor_copy, nodes[0])
        transpose_xm(d, [1])
        invert(b, nc.gpsimd)
        copy_xT(d, nc.scalar.copy, nodes[1])
        spread_norms(d)
        correlate(c)
        roots(d)
        quantise(d + X_CALL, nodes[0])
        quantise(d + X_CALL, nodes[1])
        magnitudes(c)
        scale_and_store(b)
        invert(c, nc.vector)
        invert(d, nc.vector)
        correlate(d, [0])
        correlate(d, [1])
        magnitudes(d, [0])
        magnitudes(d, [1])
        scale_and_store(c)
        scale_and_store(d, [0])
        scale_and_store(d, [1])
